import numpy as np
import ml_dtypes


def mxq(x, axis, fmt="e4m3"):
    dtype, down = {"e4m3": (ml_dtypes.float8_e4m3fn, 7), "e5m2": (ml_dtypes.float8_e5m2, 14)}[fmt]
    v = np.moveaxis(np.asarray(x, np.float32).astype(ml_dtypes.bfloat16).astype(np.float64), axis, -1)
    blocks = v.reshape(v.shape[:-1] + (-1, 32))
    amax = np.abs(blocks).max(-1, keepdims=True)
    byte = np.maximum(np.where(amax > 0, np.frexp(amax)[1] - 1 + 127, 0) - down, 1)
    scale = np.exp2(byte - 127.0)
    codes = (blocks / scale).astype(np.float32).astype(dtype).astype(np.float64)
    return np.moveaxis((codes * scale).reshape(v.shape), -1, axis)


WIDE = False


def mx_kscale(k):
    if not WIDE:
        return np.ones(k)
    levels = np.array([10, -10, 5, -5, 0])
    a = np.random.permutation(np.resize(levels, k // 512 * 4)).reshape(k // 512, 4)
    idx = np.arange(k)
    return np.exp2(a[idx // 512, idx % 128 // 32])


BF16 = ml_dtypes.bfloat16


def bf(x):
    return np.asarray(x, np.float32).astype(BF16)


def f64(x):
    return np.asarray(x).astype(np.float64)


E2M1 = np.array([0.0, 0.5, 1.0, 1.5, 2.0, 3.0, 4.0, 6.0, -0.0, -0.5, -1.0, -1.5, -2.0, -3.0, -4.0, -6.0])


def pack_weight(w, fmt):
    k, n = w.shape
    w = f64(bf(w)).reshape(k // 32, 32, n)
    amax = np.abs(w).max(1)
    if fmt == "e4m3":
        byte = np.frexp(amax)[1] - 1 + 127 - 7
    else:
        mant, ex = np.frexp(amax / 6.0)
        byte = np.where(mant > 0.5, ex, ex - 1) + 127
    byte = np.clip(np.where(amax > 0, byte, 1), 1, 254)
    scaled = (w * np.exp2(127.0 - byte)[:, None, :]).reshape(k, n).astype(np.float32)
    by_word = np.ascontiguousarray(scaled.reshape(k // 512, 128, 4, n).transpose(0, 1, 3, 2))
    if fmt == "e4m3":
        words = by_word.astype(ml_dtypes.float8_e4m3fn).view(np.uint8)
    else:
        c = by_word.astype(ml_dtypes.float4_e2m1fn).view(np.uint8) & 0xF
        words = c[..., 0::2] | (c[..., 1::2] << 4)
    return np.ascontiguousarray(words), np.ascontiguousarray(byte.astype(np.uint8).reshape(k // 512, 16, n))


def unpack_weight(words, scales, fmt):
    g, p, n, _ = words.shape
    if fmt == "e4m3":
        vals = np.ascontiguousarray(words).view(ml_dtypes.float8_e4m3fn).astype(np.float64)
    else:
        nib = np.empty((g, p, n, 4), np.uint8)
        nib[..., 0::2] = words & 0xF
        nib[..., 1::2] = words >> 4
        vals = E2M1[nib]
    vals = vals * np.repeat(np.exp2(scales.astype(np.float64) - 127.0), 8, axis=1)[..., None]
    return vals.transpose(0, 1, 3, 2).reshape(g * 512, n)


N_FFT, B, T = 3072, 16, 8
STRIDE = N_FFT + 1
L = T * STRIDE
FMT = "e4m3"


def _fourier_kernels(n_fft):
    s = np.arange(n_fft, dtype=np.float64)
    k = np.arange(n_fft, dtype=np.float64)[:, None]
    ang = 2.0 * np.pi * k * s / n_fft
    return np.sin(ang), np.cos(ang)


def setup_inputs():
    s = mx_kscale(N_FFT)
    sx = np.concatenate([s, np.ones(1)])
    x = (np.random.standard_normal((1, B, T, STRIDE)) * sx).reshape(1, B, L)
    ws, wc = _fourier_kernels(N_FFT)
    wsin = (ws + 0.5 * np.random.standard_normal((N_FFT, N_FFT))) / np.sqrt(N_FFT) / s[None, :]
    wcos = (wc + 0.5 * np.random.standard_normal((N_FFT, N_FFT))) / np.sqrt(N_FFT) / s[None, :]
    wsin_words, wsin_scales = pack_weight(np.ascontiguousarray(wsin.T), FMT)
    wcos_words, wcos_scales = pack_weight(np.ascontiguousarray(wcos.T), FMT)
    return {"x": bf(x), "wsin_words": wsin_words, "wsin_scales": wsin_scales,
            "wcos_words": wcos_words, "wcos_scales": wcos_scales}


def reference(x, wsin_words, wsin_scales, wcos_words, wcos_scales):
    sig = f64(x)[0]
    frames = sig.reshape(B, T, STRIDE)[..., :N_FFT]
    fq = mxq(frames, 2, "e4m3")
    real = np.einsum('btn,kn->tbk', fq, unpack_weight(wcos_words, wcos_scales, FMT).T)
    imag = np.einsum('btn,kn->tbk', fq, unpack_weight(wsin_words, wsin_scales, FMT).T)
    return real, -imag

@@ -1,0 +1,153 @@
+from contextlib import ExitStack
+
+import concourse.mybir as mybir
+from concourse.masks import make_identity
+
+F32 = mybir.dt.float32
+BF16 = mybir.dt.bfloat16
+U8 = mybir.dt.uint8
+U32 = mybir.dt.uint32
+I32 = mybir.dt.int32
+FP8X4 = mybir.dt.float8_e4m3fn_x4
+
+P = 128
+N_FFT = 3072
+STRIDE = N_FFT + 1
+B = 16
+T = 8
+K_PASS = 512
+GROUPS = N_FFT // K_PASS
+N_TILE = 512
+COLS = N_FFT // N_TILE
+FLOPS = 2 * 2 * P * N_FFT * N_FFT
+
+SCALE_QUEUE = "sync"
+TAIL_PIECES = 3
+
+
+def tile_dftlayer_w_kernel(tc, x, wsin_words, wsin_scales, wcos_words, wcos_scales, out_0, out_1):
+    nc = tc.nc
+    with ExitStack() as ctx:
+        ctx.enter_context(tc.manual_schedule())
+        keep = ctx.enter_context(tc.tile_pool(name="keep", bufs=1))
+        psum = ctx.enter_context(tc.psum_pool(name="psum", bufs=1))
+
+        planes = [keep.tile([P, N_FFT], U8, align_bytes=64, name="planes%d" % s) for s in range(3)]
+        x_sb = keep.tile([P, N_FFT], BF16, align_bytes=64, name="x_sb")
+        ident = keep.tile([P, P], F32, name="ident")
+        perm = keep.tile([P, P], F32, name="perm")
+        grouped = keep.tile([P, 4 * GROUPS * P], BF16, align_bytes=64, name="grouped")
+        x_codes = keep.tile([P, GROUPS * P], U32, align_bytes=64, name="x_codes")
+        x_scales = keep.tile([P, GROUPS * P], U8, align_bytes=64, name="x_scales")
+        words = {}
+        for w in ("cos", "sin"):
+            for g in range(GROUPS):
+                words[(w, g)] = keep.tile([P, N_FFT], U32, align_bytes=64, name="w_%s%d" % (w, g))
+        res = {w: keep.tile([P, N_FFT], F32, name="res_%s" % w) for w in ("cos", "sin")}
+        dram_words = {"cos": wcos_words, "sin": wsin_words}
+        dram_scales = {"cos": wcos_scales, "sin": wsin_scales}
+        dram_out = {"cos": out_0.rearrange("t b k -> (t b) k"), "sin": out_1.rearrange("t b k -> (t b) k")}
+
+        order = [("cos", g) for g in range(GROUPS)] + [("sin", g) for g in range(GROUPS)]
+        where = {wg: (i // 4, 4 * (i % 4)) for i, wg in enumerate(order)}
+
+        for s in range(3):
+            nc.vector.memset(planes[s][:].bitcast(I32), 0)
+        nc.sync.dma_start(out=x_sb[:], in_=x[0].rearrange("b (t s) -> (b t) s", s=STRIDE)[:, 0:N_FFT])
+        make_identity(nc, ident[:])
+        nc.vector.tensor_copy(
+            out=perm[:].rearrange("p (t b) -> p t b", t=T),
+            in_=ident[:].rearrange("p (b t) -> p t b", t=T),
+        )
+
+        runs = [("cos", 0, 4), ("cos", 4, 2), ("sin", 0, 2), ("sin", 2, 4)]
+        for w, g0, n in runs:
+            s, off = where[(w, g0)]
+            for q in (0, 2, 1, 3):
+                dst = planes[s][32 * q + off : 32 * q + off + 4 * n, :]
+                src = dram_scales[w][g0 : g0 + n, 4 * q : 4 * q + 4, :]
+                if SCALE_QUEUE == "sync":
+                    nc.sync.dma_start(out=dst.bitcast(I32), in_=src.bitcast(I32))
+                else:
+                    nc.gpsimd.dma_start(out=dst.bitcast(F32), in_=src.bitcast(F32))
+
+        piece = N_FFT // TAIL_PIECES
+        for w, g in order:
+            src = dram_words[w][g].rearrange("p n t -> p (n t)").bitcast(I32)
+            dst = words[(w, g)][:].bitcast(I32)
+            if (w, g) == ("sin", GROUPS - 1):
+                for c in range(TAIL_PIECES):
+                    nc.sync.dma_start(out=dst[:, c * piece : (c + 1) * piece], in_=src[:, c * piece : (c + 1) * piece])
+            else:
+                nc.sync.dma_start(out=dst, in_=src)
+
+        x_words = x_sb[:].bitcast(F32)
+        grouped_words = grouped[:].bitcast(F32)
+        banks_t = []
+        for h in range(GROUPS // 2):
+            xt = psum.tile([P, 2, 2, P], F32, tag="bank%d" % (5 + h), name="xt%d" % h)
+            banks_t.append(xt)
+            for gg in range(2):
+                g = 2 * h + gg
+                for u in range(2):
+                    nc.tensor.transpose(xt[:, gg, u, :], x_words[:, 256 * g + u : 256 * (g + 1) : 2], perm[:])
+        for h in range(GROUPS // 2):
+            dst = grouped_words[:, 512 * h : 512 * (h + 1)].rearrange("p (g m u) -> p g m u", g=2, u=2)
+            src = banks_t[h][:].rearrange("p g u m -> p g m u")
+            if h == 1:
+                nc.scalar.copy(out=dst, in_=src)
+            else:
+                nc.vector.tensor_copy(out=dst, in_=src)
+        for h in range(GROUPS // 2):
+            nc.vector.quantize_mx(
+                out=x_codes[:, 256 * h : 256 * (h + 1)].bitcast(FP8X4),
+                scales=x_scales[:, 256 * h : 256 * (h + 1)],
+                in_=grouped[:, 1024 * h : 1024 * (h + 1)],
+            )
+
+        def mx_pass(acc, w, g, j):
+            s, off = where[(w, g)]
+            nc.tensor.matmul_mx(
+                out=acc[:],
+                lhsT=x_codes[:, P * g : P * (g + 1)].bitcast(FP8X4),
+                lhsT_scale=x_scales[:, P * g : P * (g + 1)],
+                rhs=words[(w, g)][:, N_TILE * j : N_TILE * (j + 1)].bitcast(FP8X4),
+                rhs_scale=planes[s][off:P, N_TILE * j : N_TILE * (j + 1)],
+                start=(g == 0),
+                stop=(g == GROUPS - 1),
+            )
+
+        def leave(acc, w, j):
+            dst = res[w][:, N_TILE * j : N_TILE * (j + 1)]
+            if w == "cos":
+                if j % 2 == 0:
+                    nc.vector.tensor_copy(out=dst, in_=acc[:])
+                else:
+                    nc.scalar.copy(out=dst, in_=acc[:])
+            else:
+                if j % 2 == 0:
+                    nc.vector.tensor_scalar_mul(out=dst, in0=acc[:], scalar1=-1.0)
+                else:
+                    nc.scalar.mul(out=dst, in_=acc[:], mul=-1.0)
+
+        acc_cos = [psum.tile([P, N_TILE], F32, tag="bank%d" % j, name="acc_cos%d" % j) for j in range(COLS)]
+        for g in range(GROUPS):
+            for j in range(COLS):
+                mx_pass(acc_cos[j], "cos", g, j)
+        for j in range(COLS):
+            leave(acc_cos[j], "cos", j)
+
+        acc_sin = [psum.tile([P, N_TILE], F32, tag="bank%d" % ((6 + j) % 8), name="acc_sin%d" % j) for j in range(COLS)]
+        for g in range(GROUPS - 1):
+            for j in range(COLS):
+                mx_pass(acc_sin[j], "sin", g, j)
+        nc.sync.dma_start(out=dram_out["cos"], in_=res["cos"][:])
+        per = COLS // TAIL_PIECES
+        for c in range(TAIL_PIECES):
+            for j in range(per * c, per * (c + 1)):
+                mx_pass(acc_sin[j], "sin", GROUPS - 1, j)
+            for j in range(per * c, per * (c + 1)):
+                leave(acc_sin[j], "sin", j)
+            nc.sync.dma_start(
+                out=dram_out["sin"][:, c * piece : (c + 1) * piece], in_=res["sin"][:, c * piece : (c + 1) * piece]
+            )

@@ -21,7 +21,7 @@ N_TILE = 512
 COLS = N_FFT // N_TILE
 FLOPS = 2 * 2 * P * N_FFT * N_FFT
 
-SCALE_QUEUE = "sync"
+SCALE_QUEUE = "gpsimd"
 TAIL_PIECES = 3
 
 

@@ -21,7 +21,7 @@ N_TILE = 512
 COLS = N_FFT // N_TILE
 FLOPS = 2 * 2 * P * N_FFT * N_FFT
 
-SCALE_QUEUE = "gpsimd"
+SCALE_QUEUE = "sync"
 TAIL_PIECES = 3
 
 
@@ -32,7 +32,7 @@ def tile_dftlayer_w_kernel(tc, x, wsin_words, wsin_scales, wcos_words, wcos_scal
         keep = ctx.enter_context(tc.tile_pool(name="keep", bufs=1))
         psum = ctx.enter_context(tc.psum_pool(name="psum", bufs=1))
 
-        planes = [keep.tile([P, N_FFT], U8, align_bytes=64, name="planes%d" % s) for s in range(3)]
+        planes = [keep.tile([P, N_FFT], U8, align_bytes=64, name="planes%d" % s) for s in range(4)]
         x_sb = keep.tile([P, N_FFT], BF16, align_bytes=64, name="x_sb")
         ident = keep.tile([P, P], F32, name="ident")
         perm = keep.tile([P, P], F32, name="perm")
@@ -49,9 +49,9 @@ def tile_dftlayer_w_kernel(tc, x, wsin_words, wsin_scales, wcos_words, wcos_scal
         dram_out = {"cos": out_0.rearrange("t b k -> (t b) k"), "sin": out_1.rearrange("t b k -> (t b) k")}
 
         order = [("cos", g) for g in range(GROUPS)] + [("sin", g) for g in range(GROUPS)]
-        where = {wg: (i // 4, 4 * (i % 4)) for i, wg in enumerate(order)}
+        where = {(w, g): (2 * wi + g // 4, 4 * (g % 4)) for wi, w in enumerate(("cos", "sin")) for g in range(GROUPS)}
 
-        for s in range(3):
+        for s in range(4):
             nc.vector.memset(planes[s][:].bitcast(I32), 0)
         nc.sync.dma_start(out=x_sb[:], in_=x[0].rearrange("b (t s) -> (b t) s", s=STRIDE)[:, 0:N_FFT])
         make_identity(nc, ident[:])
@@ -60,10 +60,10 @@ def tile_dftlayer_w_kernel(tc, x, wsin_words, wsin_scales, wcos_words, wcos_scal
             in_=ident[:].rearrange("p (b t) -> p t b", t=T),
         )
 
-        runs = [("cos", 0, 4), ("cos", 4, 2), ("sin", 0, 2), ("sin", 2, 4)]
-        for w, g0, n in runs:
+        runs = [("cos", 0, 4), ("cos", 4, 2), ("sin", 0, 4), ("sin", 4, 2)]
+        for q, w, g0, n in [(q, w, g0, n) for half in ((2, 3), (0, 1)) for (w, g0, n) in runs for q in half]:
             s, off = where[(w, g0)]
-            for q in (0, 2, 1, 3):
+            for once in (0,):
                 dst = planes[s][32 * q + off : 32 * q + off + 4 * n, :]
                 src = dram_scales[w][g0 : g0 + n, 4 * q : 4 * q + 4, :]
                 if SCALE_QUEUE == "sync":

@@ -21,8 +21,10 @@ N_TILE = 512
 COLS = N_FFT // N_TILE
 FLOPS = 2 * 2 * P * N_FFT * N_FFT
 
-SCALE_QUEUE = "sync"
 TAIL_PIECES = 3
+PACKED = 4
+QUARTER = N_FFT // 4
+N_HALF = 256
 
 
 def tile_dftlayer_w_kernel(tc, x, wsin_words, wsin_scales, wcos_words, wcos_scales, out_0, out_1):
@@ -32,7 +34,8 @@ def tile_dftlayer_w_kernel(tc, x, wsin_words, wsin_scales, wcos_words, wcos_scal
         keep = ctx.enter_context(tc.tile_pool(name="keep", bufs=1))
         psum = ctx.enter_context(tc.psum_pool(name="psum", bufs=1))
 
-        planes = [keep.tile([P, N_FFT], U8, align_bytes=64, name="planes%d" % s) for s in range(4)]
+        planes = {w: keep.tile([P, N_FFT], U8, align_bytes=64, name="planes_%s" % w) for w in ("cos", "sin")}
+        rest = {w: keep.tile([P, 2 * QUARTER], U8, align_bytes=64, name="rest_%s" % w) for w in ("cos", "sin")}
         x_sb = keep.tile([P, N_FFT], BF16, align_bytes=64, name="x_sb")
         ident = keep.tile([P, P], F32, name="ident")
         perm = keep.tile([P, P], F32, name="perm")
@@ -49,10 +52,10 @@ def tile_dftlayer_w_kernel(tc, x, wsin_words, wsin_scales, wcos_words, wcos_scal
         dram_out = {"cos": out_0.rearrange("t b k -> (t b) k"), "sin": out_1.rearrange("t b k -> (t b) k")}
 
         order = [("cos", g) for g in range(GROUPS)] + [("sin", g) for g in range(GROUPS)]
-        where = {(w, g): (2 * wi + g // 4, 4 * (g % 4)) for wi, w in enumerate(("cos", "sin")) for g in range(GROUPS)}
 
-        for s in range(4):
-            nc.vector.memset(planes[s][:].bitcast(I32), 0)
+        for w in ("cos", "sin"):
+            nc.vector.memset(planes[w][:].bitcast(I32), 0)
+            nc.vector.memset(rest[w][:].bitcast(I32), 0)
         nc.sync.dma_start(out=x_sb[:], in_=x[0].rearrange("b (t s) -> (b t) s", s=STRIDE)[:, 0:N_FFT])
         make_identity(nc, ident[:])
         nc.vector.tensor_copy(
@@ -60,16 +63,20 @@ def tile_dftlayer_w_kernel(tc, x, wsin_words, wsin_scales, wcos_words, wcos_scal
             in_=ident[:].rearrange("p (b t) -> p t b", t=T),
         )
 
-        runs = [("cos", 0, 4), ("cos", 4, 2), ("sin", 0, 4), ("sin", 4, 2)]
-        for q, w, g0, n in [(q, w, g0, n) for half in ((2, 3), (0, 1)) for (w, g0, n) in runs for q in half]:
-            s, off = where[(w, g0)]
-            for once in (0,):
-                dst = planes[s][32 * q + off : 32 * q + off + 4 * n, :]
-                src = dram_scales[w][g0 : g0 + n, 4 * q : 4 * q + 4, :]
-                if SCALE_QUEUE == "sync":
-                    nc.sync.dma_start(out=dst.bitcast(I32), in_=src.bitcast(I32))
-                else:
-                    nc.gpsimd.dma_start(out=dst.bitcast(F32), in_=src.bitcast(F32))
+        for half in ((2, 3), (0, 1)):
+            for w in ("cos", "sin"):
+                for q in half:
+                    rows = slice(4 * q, 4 * q + 4)
+                    nc.sync.dma_start(
+                        out=planes[w][32 * q : 32 * q + 16, :].bitcast(I32),
+                        in_=dram_scales[w][0:PACKED, rows, :].bitcast(I32),
+                    )
+                    for g in range(PACKED, GROUPS):
+                        c0 = (g - PACKED) * QUARTER
+                        nc.sync.dma_start(
+                            out=rest[w][32 * q : 32 * q + 16, c0 : c0 + QUARTER].bitcast(I32),
+                            in_=dram_scales[w][g, rows, :].bitcast(I32).rearrange("i (c n) -> c i n", c=4),
+                        )
 
         piece = N_FFT // TAIL_PIECES
         for w, g in order:
@@ -105,17 +112,34 @@ def tile_dftlayer_w_kernel(tc, x, wsin_words, wsin_scales, wcos_words, wcos_scal
                 in_=grouped[:, 1024 * h : 1024 * (h + 1)],
             )
 
-        def mx_pass(acc, w, g, j):
-            s, off = where[(w, g)]
+        def mx_call(out, w, g, cols, plane, last):
             nc.tensor.matmul_mx(
-                out=acc[:],
+                out=out,
                 lhsT=x_codes[:, P * g : P * (g + 1)].bitcast(FP8X4),
                 lhsT_scale=x_scales[:, P * g : P * (g + 1)],
-                rhs=words[(w, g)][:, N_TILE * j : N_TILE * (j + 1)].bitcast(FP8X4),
-                rhs_scale=planes[s][off:P, N_TILE * j : N_TILE * (j + 1)],
+                rhs=words[(w, g)][:, cols].bitcast(FP8X4),
+                rhs_scale=plane,
                 start=(g == 0),
-                stop=(g == GROUPS - 1),
+                stop=last,
             )
+
+        def mx_pass(acc, w, g, j):
+            if g < PACKED:
+                cols = slice(N_TILE * j, N_TILE * (j + 1))
+                mx_call(acc[:], w, g, cols, planes[w][4 * g : P, cols], False)
+                return
+            for b in range(N_TILE // N_HALF):
+                n0 = N_TILE * j + N_HALF * b
+                c, n = divmod(n0, QUARTER)
+                n += (g - PACKED) * QUARTER
+                mx_call(
+                    acc[:, N_HALF * b : N_HALF * (b + 1)],
+                    w,
+                    g,
+                    slice(n0, n0 + N_HALF),
+                    rest[w][4 * c : P, n : n + N_HALF],
+                    g == GROUPS - 1 and b == 1,
+                )
 
         def leave(acc, w, j):
             dst = res[w][:, N_TILE * j : N_TILE * (j + 1)]

@@ -63,23 +63,22 @@ def tile_dftlayer_w_kernel(tc, x, wsin_words, wsin_scales, wcos_words, wcos_scal
             in_=ident[:].rearrange("p (b t) -> p t b", t=T),
         )
 
-        for half in ((2, 3), (0, 1)):
-            for w in ("cos", "sin"):
-                for q in half:
-                    rows = slice(4 * q, 4 * q + 4)
-                    nc.sync.dma_start(
-                        out=planes[w][32 * q : 32 * q + 16, :].bitcast(I32),
-                        in_=dram_scales[w][0:PACKED, rows, :].bitcast(I32),
-                    )
-                    for g in range(PACKED, GROUPS):
-                        c0 = (g - PACKED) * QUARTER
-                        nc.sync.dma_start(
-                            out=rest[w][32 * q : 32 * q + 16, c0 : c0 + QUARTER].bitcast(I32),
-                            in_=dram_scales[w][g, rows, :].bitcast(I32).rearrange("i (c n) -> c i n", c=4),
-                        )
+        def load_packed(w, q):
+            nc.sync.dma_start(
+                out=planes[w][32 * q : 32 * q + 16, :].bitcast(I32),
+                in_=dram_scales[w][0:PACKED, 4 * q : 4 * q + 4, :].bitcast(I32),
+            )
+
+        def load_rest(w, q, g):
+            c0 = (g - PACKED) * QUARTER
+            nc.sync.dma_start(
+                out=rest[w][32 * q : 32 * q + 16, c0 : c0 + QUARTER].bitcast(I32),
+                in_=dram_scales[w][g, 4 * q : 4 * q + 4, :].bitcast(I32).rearrange("i (c n) -> c i n", c=4),
+            )
 
         piece = N_FFT // TAIL_PIECES
-        for w, g in order:
+
+        def load_words(w, g):
             src = dram_words[w][g].rearrange("p n t -> p (n t)").bitcast(I32)
             dst = words[(w, g)][:].bitcast(I32)
             if (w, g) == ("sin", GROUPS - 1):
@@ -87,6 +86,28 @@ def tile_dftlayer_w_kernel(tc, x, wsin_words, wsin_scales, wcos_words, wcos_scal
                     nc.sync.dma_start(out=dst[:, c * piece : (c + 1) * piece], in_=src[:, c * piece : (c + 1) * piece])
             else:
                 nc.sync.dma_start(out=dst, in_=src)
+
+        def load_rests(w, q):
+            for g in range(PACKED, GROUPS):
+                load_rest(w, q, g)
+
+        load_packed("cos", 2)
+        load_packed("cos", 3)
+        load_rests("cos", 2)
+        load_packed("sin", 2)
+        load_packed("sin", 3)
+        load_rests("cos", 3)
+        load_packed("cos", 0)
+        load_rests("sin", 2)
+        load_packed("cos", 1)
+        load_rests("sin", 3)
+        load_packed("sin", 0)
+        load_packed("sin", 1)
+        behind = [("cos", 0), ("cos", 1), ("sin", 0), ("sin", 1)]
+        for n, (w, g) in enumerate(order):
+            load_words(w, g)
+            if n < len(behind):
+                load_rests(*behind[n])
 
         x_words = x_sb[:].bitcast(F32)
         grouped_words = grouped[:].bitcast(F32)

from contextlib import ExitStack

import concourse.mybir as mybir
from concourse.masks import make_identity

F32 = mybir.dt.float32
BF16 = mybir.dt.bfloat16
U8 = mybir.dt.uint8
U32 = mybir.dt.uint32
I32 = mybir.dt.int32
FP8X4 = mybir.dt.float8_e4m3fn_x4

P = 128
N_FFT = 3072
STRIDE = N_FFT + 1
B = 16
T = 8
K_PASS = 512
GROUPS = N_FFT // K_PASS
N_TILE = 512
COLS = N_FFT // N_TILE
FLOPS = 2 * 2 * P * N_FFT * N_FFT

TAIL_PIECES = 3
PACKED = 4
QUARTER = N_FFT // 4
N_HALF = 256


def tile_dftlayer_w_kernel(tc, x, wsin_words, wsin_scales, wcos_words, wcos_scales, out_0, out_1):
    nc = tc.nc
    with ExitStack() as ctx:
        ctx.enter_context(tc.manual_schedule())
        keep = ctx.enter_context(tc.tile_pool(name="keep", bufs=1))
        psum = ctx.enter_context(tc.psum_pool(name="psum", bufs=1))

        planes = {w: keep.tile([P, N_FFT], U8, align_bytes=64, name="planes_%s" % w) for w in ("cos", "sin")}
        rest = {w: keep.tile([P, 2 * QUARTER], U8, align_bytes=64, name="rest_%s" % w) for w in ("cos", "sin")}
        x_sb = keep.tile([P, N_FFT], BF16, align_bytes=64, name="x_sb")
        ident = keep.tile([P, P], F32, name="ident")
        perm = keep.tile([P, P], F32, name="perm")
        grouped = keep.tile([P, 4 * GROUPS * P], BF16, align_bytes=64, name="grouped")
        x_codes = keep.tile([P, GROUPS * P], U32, align_bytes=64, name="x_codes")
        x_scales = keep.tile([P, GROUPS * P], U8, align_bytes=64, name="x_scales")
        words = {}
        for w in ("cos", "sin"):
            for g in range(GROUPS):
                words[(w, g)] = keep.tile([P, N_FFT], U32, align_bytes=64, name="w_%s%d" % (w, g))
        res = {w: keep.tile([P, N_FFT], F32, name="res_%s" % w) for w in ("cos", "sin")}
        dram_words = {"cos": wcos_words, "sin": wsin_words}
        dram_scales = {"cos": wcos_scales, "sin": wsin_scales}
        dram_out = {"cos": out_0.rearrange("t b k -> (t b) k"), "sin": out_1.rearrange("t b k -> (t b) k")}

        order = [("cos", g) for g in range(GROUPS)] + [("sin", g) for g in range(GROUPS)]

        for w in ("cos", "sin"):
            nc.vector.memset(planes[w][:].bitcast(I32), 0)
            nc.vector.memset(rest[w][:].bitcast(I32), 0)
        nc.sync.dma_start(out=x_sb[:], in_=x[0].rearrange("b (t s) -> (b t) s", s=STRIDE)[:, 0:N_FFT])
        make_identity(nc, ident[:])
        nc.vector.tensor_copy(
            out=perm[:].rearrange("p (t b) -> p t b", t=T),
            in_=ident[:].rearrange("p (b t) -> p t b", t=T),
        )

        def load_packed(w, q):
            nc.sync.dma_start(
                out=planes[w][32 * q : 32 * q + 16, :].bitcast(I32),
                in_=dram_scales[w][0:PACKED, 4 * q : 4 * q + 4, :].bitcast(I32),
            )

        def load_rest(w, q, g):
            c0 = (g - PACKED) * QUARTER
            nc.sync.dma_start(
                out=rest[w][32 * q : 32 * q + 16, c0 : c0 + QUARTER].bitcast(I32),
                in_=dram_scales[w][g, 4 * q : 4 * q + 4, :].bitcast(I32).rearrange("i (c n) -> c i n", c=4),
            )

        piece = N_FFT // TAIL_PIECES

        def load_words(w, g):
            src = dram_words[w][g].rearrange("p n t -> p (n t)").bitcast(I32)
            dst = words[(w, g)][:].bitcast(I32)
            if (w, g) == ("sin", GROUPS - 1):
                for c in range(TAIL_PIECES):
                    nc.sync.dma_start(out=dst[:, c * piece : (c + 1) * piece], in_=src[:, c * piece : (c + 1) * piece])
            else:
                nc.sync.dma_start(out=dst, in_=src)

        def load_rests(w, q):
            for g in range(PACKED, GROUPS):
                load_rest(w, q, g)

        load_packed("cos", 2)
        load_packed("cos", 3)
        load_rests("cos", 2)
        load_packed("sin", 2)
        load_packed("sin", 3)
        load_rests("cos", 3)
        load_packed("cos", 0)
        load_rests("sin", 2)
        load_packed("cos", 1)
        load_rests("sin", 3)
        load_packed("sin", 0)
        load_packed("sin", 1)
        behind = [("cos", 0), ("cos", 1), ("sin", 0), ("sin", 1)]
        for n, (w, g) in enumerate(order):
            load_words(w, g)
            if n < len(behind):
                load_rests(*behind[n])

        x_words = x_sb[:].bitcast(F32)
        grouped_words = grouped[:].bitcast(F32)
        banks_t = []
        for h in range(GROUPS // 2):
            xt = psum.tile([P, 2, 2, P], F32, tag="bank%d" % (5 + h), name="xt%d" % h)
            banks_t.append(xt)
            for gg in range(2):
                g = 2 * h + gg
                for u in range(2):
                    nc.tensor.transpose(xt[:, gg, u, :], x_words[:, 256 * g + u : 256 * (g + 1) : 2], perm[:])
        for h in range(GROUPS // 2):
            dst = grouped_words[:, 512 * h : 512 * (h + 1)].rearrange("p (g m u) -> p g m u", g=2, u=2)
            src = banks_t[h][:].rearrange("p g u m -> p g m u")
            if h == 1:
                nc.scalar.copy(out=dst, in_=src)
            else:
                nc.vector.tensor_copy(out=dst, in_=src)
        for h in range(GROUPS // 2):
            nc.vector.quantize_mx(
                out=x_codes[:, 256 * h : 256 * (h + 1)].bitcast(FP8X4),
                scales=x_scales[:, 256 * h : 256 * (h + 1)],
                in_=grouped[:, 1024 * h : 1024 * (h + 1)],
            )

        def mx_call(out, w, g, cols, plane, last):
            nc.tensor.matmul_mx(
                out=out,
                lhsT=x_codes[:, P * g : P * (g + 1)].bitcast(FP8X4),
                lhsT_scale=x_scales[:, P * g : P * (g + 1)],
                rhs=words[(w, g)][:, cols].bitcast(FP8X4),
                rhs_scale=plane,
                start=(g == 0),
                stop=last,
            )

        def mx_pass(acc, w, g, j):
            if g < PACKED:
                cols = slice(N_TILE * j, N_TILE * (j + 1))
                mx_call(acc[:], w, g, cols, planes[w][4 * g : P, cols], False)
                return
            for b in range(N_TILE // N_HALF):
                n0 = N_TILE * j + N_HALF * b
                c, n = divmod(n0, QUARTER)
                n += (g - PACKED) * QUARTER
                mx_call(
                    acc[:, N_HALF * b : N_HALF * (b + 1)],
                    w,
                    g,
                    slice(n0, n0 + N_HALF),
                    rest[w][4 * c : P, n : n + N_HALF],
                    g == GROUPS - 1 and b == 1,
                )

        def leave(acc, w, j):
            dst = res[w][:, N_TILE * j : N_TILE * (j + 1)]
            if w == "cos":
                if j % 2 == 0:
                    nc.vector.tensor_copy(out=dst, in_=acc[:])
                else:
                    nc.scalar.copy(out=dst, in_=acc[:])
            else:
                if j % 2 == 0:
                    nc.vector.tensor_scalar_mul(out=dst, in0=acc[:], scalar1=-1.0)
                else:
                    nc.scalar.mul(out=dst, in_=acc[:], mul=-1.0)

        acc_cos = [psum.tile([P, N_TILE], F32, tag="bank%d" % j, name="acc_cos%d" % j) for j in range(COLS)]
        for g in range(GROUPS):
            for j in range(COLS):
                mx_pass(acc_cos[j], "cos", g, j)
        for j in range(COLS):
            leave(acc_cos[j], "cos", j)

        acc_sin = [psum.tile([P, N_TILE], F32, tag="bank%d" % ((6 + j) % 8), name="acc_sin%d" % j) for j in range(COLS)]
        for g in range(GROUPS - 1):
            for j in range(COLS):
                mx_pass(acc_sin[j], "sin", g, j)
        nc.sync.dma_start(out=dram_out["cos"], in_=res["cos"][:])
        per = COLS // TAIL_PIECES
        for c in range(TAIL_PIECES):
            for j in range(per * c, per * (c + 1)):
                mx_pass(acc_sin[j], "sin", GROUPS - 1, j)
            for j in range(per * c, per * (c + 1)):
                leave(acc_sin[j], "sin", j)
            nc.sync.dma_start(
                out=dram_out["sin"][:, c * piece : (c + 1) * piece], in_=res["sin"][:, c * piece : (c + 1) * piece]
            )
